import numpy as np
import ml_dtypes


def mxq(x, axis, fmt="e4m3"):
    dtype, down = {"e4m3": (ml_dtypes.float8_e4m3fn, 7), "e5m2": (ml_dtypes.float8_e5m2, 14)}[fmt]
    v = np.moveaxis(np.asarray(x, np.float32).astype(ml_dtypes.bfloat16).astype(np.float64), axis, -1)
    blocks = v.reshape(v.shape[:-1] + (-1, 32))
    amax = np.abs(blocks).max(-1, keepdims=True)
    byte = np.maximum(np.where(amax > 0, np.frexp(amax)[1] - 1 + 127, 0) - down, 1)
    scale = np.exp2(byte - 127.0)
    codes = (blocks / scale).astype(np.float32).astype(dtype).astype(np.float64)
    return np.moveaxis((codes * scale).reshape(v.shape), -1, axis)


WIDE = False


def mx_kscale(k):
    if not WIDE:
        return np.ones(k)
    levels = np.array([10, -10, 5, -5, 0])
    if k % 512:
        return np.exp2(np.random.permutation(np.resize(levels, k // 32))).repeat(32)
    a = np.empty((k // 512, 16))
    for p in range(k // 512):
        a[p, :8] = np.random.permutation(np.resize(levels, 8))
        for g in range(8):
            far = levels[np.abs(levels - a[p, g]) >= 10]
            a[p, g + 8] = far[np.random.randint(len(far))]
    return np.exp2(a.ravel()).repeat(32)


BF16 = ml_dtypes.bfloat16


def bf(x):
    return np.asarray(x, np.float32).astype(BF16)


def f64(x):
    return np.asarray(x).astype(np.float64)


B, S, D, F, P, NQ = 2, 128, 1024, 1024, 1024, 3
LN_EPS = 1e-5


def layernorm(v, g, b):
    m = v.mean(-1, keepdims=True)
    var = v.var(-1, keepdims=True)
    return (v - m) / np.sqrt(var + LN_EPS) * g + b


def draw0():
    s = mx_kscale(P)
    return {"in_proto": bf(np.random.standard_normal((NQ, F, P)) * s),
            "pt_w": bf(np.random.standard_normal((NQ, D, P)) / np.sqrt(P) / s),
            "pln_g": bf(1.0 + 0.1 * np.random.standard_normal((NQ, D))),
            "pln_b": bf(0.1 * np.random.standard_normal((NQ, D))),
            "proto_w": bf(np.random.standard_normal((NQ, F, D)) * 0.5)}


def core(in_proto, pt_w, pln_g, pln_b, proto_w):
    prc = mxq(f64(in_proto), 2, "e4m3") @ mxq(f64(pt_w), 2, "e4m3").transpose(0, 2, 1)
    return f64(proto_w) + layernorm(prc, f64(pln_g)[:, None, :], f64(pln_b)[:, None, :])


def e4m3fn_bytes(y):
    return np.clip(np.asarray(y, np.float64), -448.0, 448.0).astype(np.float32).astype(ml_dtypes.float8_e4m3fn).view(np.uint8)


def e4m3fn_values(b):
    return np.asarray(b, np.uint8).view(ml_dtypes.float8_e4m3fn).astype(np.float64)


def setup_inputs():
    d = draw0()
    x0 = np.asarray(d['pt_w']).astype(np.float64)
    s = (np.max(np.abs(x0), axis=(0, 1), keepdims=True) / 448.0).astype(np.float32)
    out = {}
    for k, v in d.items():
        if k == 'pt_w':
            out['pt_w_bytes'] = e4m3fn_bytes(x0 / s.astype(np.float64))
            out['pt_w_scale'] = s
        else:
            out[k] = v
    return out


def reference(in_proto, pt_w_bytes, pt_w_scale, pln_g, pln_b, proto_w):
    return core(in_proto, e4m3fn_values(pt_w_bytes) * pt_w_scale.astype(np.float64), pln_g, pln_b, proto_w)

@@ -1,0 +1,292 @@
+from contextlib import ExitStack
+
+import concourse.mybir as mybir
+from concourse.masks import make_identity
+
+NB, F, D, K = 3, 1024, 1024, 1024
+FLOPS = 2 * NB * F * D * K
+LN_EPS = 1e-5
+
+F32 = mybir.dt.float32
+BF16 = mybir.dt.bfloat16
+U32 = mybir.dt.uint32
+U8 = mybir.dt.uint8
+FP8 = mybir.dt.float8_e4m3fn
+FP8X4 = mybir.dt.float8_e4m3fn_x4
+ALU = mybir.AluOpType
+ACT = mybir.ActivationFunctionType
+
+P = 128
+HALF = 512
+N_STEPS = NB * 8
+N_ITEMS = NB * 8
+LATE = 12
+HALF_MEAN_SCALE = -1.0 / (32 * HALF)
+ITEM_LEAD = 12
+LOAD_LEAD = 4
+
+
+def tile_moietransformerblock_pb_kernel(tc, in_proto, pt_w_bytes, pt_w_scale, pln_g, pln_b, proto_w, out):
+    nc = tc.nc
+    with ExitStack() as ctx:
+        const = ctx.enter_context(tc.tile_pool(name="const", bufs=1))
+        raw = ctx.enter_context(tc.tile_pool(name="raw", bufs=4))
+        work = ctx.enter_context(tc.tile_pool(name="work", bufs=3))
+        quant = ctx.enter_context(tc.tile_pool(name="quant", bufs=4))
+        epi = ctx.enter_context(tc.tile_pool(name="epi", bufs=3))
+        small = ctx.enter_context(tc.tile_pool(name="small", bufs=6))
+        tps = ctx.enter_context(tc.psum_pool(name="tps", bufs=2))
+        cps = ctx.enter_context(tc.psum_pool(name="cps", bufs=2))
+        xps = ctx.enter_context(tc.psum_pool(name="xps", bufs=2))
+        ctx.enter_context(tc.manual_schedule())
+
+        scale_bc = const.tile([P, K], F32, name="scale_bc")
+        g_bc = const.tile([P, NB * D], BF16, name="g_bc")
+        b_bc = const.tile([P, NB * D], BF16, name="b_bc")
+        b_rows = const.tile([P, P], BF16, name="b_rows")
+        b_col = const.tile([P, NB * 8], F32, name="b_col")
+        ident = const.tile([P, P], F32, name="ident")
+        ident_bf = const.tile([P, P], BF16, name="ident_bf")
+        sel0 = const.tile([P, P], BF16, name="sel0")
+        one = const.tile([P, 1], F32, name="one")
+        warm = const.tile([P, 1], F32, name="warm")
+
+        raw_tiles = {}
+        wide_tiles = {}
+        tp_tiles = {}
+        grouped = {}
+        codes = {}
+        pw_tiles = {}
+        cy_tiles = {}
+        c_tiles = {}
+        x_tiles = {}
+        t_tiles = {}
+        stat_tiles = {}
+        sum_tiles = {}
+
+        def load_pairs(k):
+            if k >= N_ITEMS or k % 2 == 1:
+                return
+            n, i = divmod(k, 8)
+            rows = slice(P * i, P * (i + 2))
+            wt = raw.tile([P, 2, K], U8, name="w_bytes", tag="w_bytes")
+            nc.sync.dma_start(out=wt[:], in_=pt_w_bytes[n, rows, :].rearrange("(i p) k -> p i k", p=P))
+            at = raw.tile([P, 2, K], BF16, name="a_raw", tag="a_raw")
+            nc.sync.dma_start(out=at[:], in_=in_proto[n, rows, :].rearrange("(i p) k -> p i k", p=P))
+            raw_tiles[("w", k)] = wt
+            raw_tiles[("a", k)] = at
+
+        def widen(k):
+            if k >= N_ITEMS:
+                return
+            wide = work.tile([P, K], BF16, name="w_wide", tag="w_wide")
+            nc.vector.tensor_tensor(out=wide[:], in0=raw_tiles[("w", k - k % 2)][:, k % 2, :].bitcast(FP8), in1=scale_bc[:], op=ALU.mult)
+            wide_tiles[k] = wide
+
+        def transp(k, ops=("a", "w")):
+            if k >= N_ITEMS:
+                return
+            for op in ops:
+                src = wide_tiles[k][:] if op == "w" else raw_tiles[("a", k - k % 2)][:, k % 2, :]
+                words = src.bitcast(F32)
+                tp = tps.tile([P, 2, 2, P], F32, name="tp", tag="tp")
+                for g in range(2):
+                    for u in range(2):
+                        nc.tensor.transpose(tp[:, g, u, :], words[:, 256 * g + u : 256 * (g + 1) : 2], ident[:])
+                tp_tiles[(op, k)] = tp
+
+        def evac(k):
+            if k >= N_ITEMS:
+                return
+            n, i = divmod(k, 8)
+            h, ii = divmod(i, 4)
+            for op in ("a", "w"):
+                if ii == 0:
+                    grouped[(op, n, h)] = work.tile([P, 2 * 2048], BF16, name="grouped", tag="grouped", bufs=4, align_bytes=64)
+                grp = grouped[(op, n, h)]
+                nc.scalar.copy(
+                    out=grp[:].bitcast(F32).rearrange("p (g r u) -> p g r u", g=2, u=2)[:, :, P * ii : P * (ii + 1), :],
+                    in_=tp_tiles[(op, k)][:].rearrange("p g u r -> p g r u"),
+                )
+
+        def quantise(op, k):
+            if k < 0 or k >= N_ITEMS or k % 4 != 3:
+                return
+            n, i = divmod(k, 8)
+            h = i // 4
+            cd = quant.tile([P, 1024], U32, name=op + "_codes", tag=op + "_codes", align_bytes=64)
+            sc = quant.tile([P, 1024], U8, name=op + "_scales", tag=op + "_scales", align_bytes=64)
+            nc.vector.quantize_mx(out=cd[:].bitcast(FP8X4), scales=sc[:], in_=grouped[(op, n, h)][:])
+            codes[(op, n, h)] = (cd, sc)
+
+        def load_pw(s):
+            if s >= N_STEPS:
+                return
+            n, m = divmod(s, 8)
+            t = raw.tile([P, D], BF16, name="pw", tag="pw", bufs=6)
+            nc.sync.dma_start(out=t[:], in_=proto_w[n, P * m : P * (m + 1), :])
+            pw_tiles[s] = t
+
+        def mx(s):
+            if s >= N_STEPS:
+                return
+            n, m = divmod(s, 8)
+            hf, mm = divmod(m, 4)
+            a_cd, a_sc = codes[("a", n, hf)]
+            x = xps.tile([P, D], F32, name="x", tag="x")
+            for h in range(2):
+                w_cd, w_sc = codes[("w", n, h)]
+                for g in range(2):
+                    a_cols = slice(HALF * g + P * mm, HALF * g + P * (mm + 1))
+                    w_cols = slice(HALF * g, HALF * (g + 1))
+                    nc.tensor.matmul_mx(
+                        out=x[:, HALF * h : HALF * (h + 1)],
+                        lhsT=a_cd[:, a_cols].bitcast(FP8X4),
+                        lhsT_scale=a_sc[:, a_cols],
+                        rhs=w_cd[:, w_cols].bitcast(FP8X4),
+                        rhs_scale=w_sc[:, w_cols],
+                        start=(g == 0),
+                        stop=(g == 1),
+                    )
+            x_tiles[s] = x
+
+        def stats(t):
+            def pass_over(h, func, scale, bias, col):
+                if t < N_STEPS:
+                    junk = work.tile([P, HALF], BF16, name="junk", tag="junk")
+                    nc.scalar.activation(out=junk[:], in_=x_tiles[t][:, HALF * h : HALF * (h + 1)], func=func, scale=scale, bias=bias, accum_out=sum_tiles[t][:, col : col + 1])
+
+            if t < N_STEPS:
+                sum_tiles[t] = small.tile([P, 4], F32, name="sums", tag="sums")
+                stat_tiles[t] = small.tile([P, 6], F32, name="stat", tag="stat")
+                sums, stat = sum_tiles[t], stat_tiles[t]
+            if 0 <= t - 1 < N_STEPS:
+                psums, pstat = sum_tiles[t - 1], stat_tiles[t - 1]
+            pass_over(0, ACT.Copy, HALF_MEAN_SCALE, 0.0, 0)
+            if 0 <= t - 1 < N_STEPS:
+                nc.scalar.activation(out=pstat[:, 3:4], in_=psums[:, 3:4], func=ACT.Copy, scale=1.0, bias=LN_EPS)
+                nc.scalar.activation(out=pstat[:, 4:5], in_=psums[:, 2:3], func=ACT.Identity, bias=pstat[:, 2:3])
+            pass_over(1, ACT.Copy, HALF_MEAN_SCALE, 0.0, 1)
+            if 0 <= t - 1 < N_STEPS:
+                nc.scalar.activation(out=pstat[:, 5:6], in_=pstat[:, 3:4], func=ACT.Abs_reciprocal_sqrt, bias=pstat[:, 4:5])
+            if t < N_STEPS:
+                pass_over(0, ACT.Square, 1.0 / 32, sums[:, 0:1], 2)
+                nc.scalar.activation(out=stat[:, 0:1], in_=sums[:, 1:2], func=ACT.Copy, scale=16.0)
+                pass_over(1, ACT.Square, 1.0 / 32, sums[:, 1:2], 3)
+                nc.scalar.activation(out=stat[:, 1:2], in_=sums[:, 0:1], func=ACT.Identity, scale=16.0, bias=stat[:, 0:1])
+                nc.scalar.activation(out=stat[:, 2:3], in_=sums[:, 0:1], func=ACT.Square, scale=-16.0, bias=stat[:, 0:1])
+
+        def c_pe(s):
+            if s >= N_STEPS:
+                return
+            n = s // 8
+            c = cps.tile([P, HALF], F32, name="c", tag="c")
+            c_tiles[(s, 1)] = c
+            nc.tensor.matmul(out=c[:], lhsT=ident_bf[:], rhs=pw_tiles[s][:, HALF:D], start=True, stop=False)
+            if s < LATE:
+                nc.tensor.matmul(out=c[:], lhsT=sel0[:], rhs=b_bc[:, D * n + HALF : D * (n + 1)], start=False, stop=True)
+            else:
+                for jj in range(4):
+                    col = 8 * n + 4 + jj
+                    nc.tensor.matmul(
+                        out=c[:, P * jj : P * (jj + 1)],
+                        lhsT=b_col[:, col : col + 1].to_broadcast([P, P]),
+                        rhs=ident[:],
+                        is_transpose=True,
+                        start=False,
+                        stop=(jj == 3),
+                    )
+
+        def c_g(s):
+            if s >= N_STEPS:
+                return
+            n = s // 8
+            c = epi.tile([P, HALF], F32, name="cg", tag="cg", bufs=2)
+            c_tiles[(s, 0)] = c
+            nc.gpsimd.tensor_tensor(out=c[:], in0=pw_tiles[s][:, 0:HALF], in1=b_bc[:, D * n : D * n + HALF], op=ALU.add)
+
+        def epi1(s):
+            n = s // 8
+            x = x_tiles[s]
+            stat = stat_tiles[s]
+            rstd = stat[:, 5:6]
+            t = epi.tile([P, D], F32, name="t", tag="t")
+            for h in range(2):
+                cols = slice(HALF * h, HALF * (h + 1))
+                nc.vector.scalar_tensor_tensor(out=t[:, cols], in0=x[:, cols], scalar=stat[:, 1:2], in1=g_bc[:, D * n + HALF * h : D * n + HALF * (h + 1)], op0=ALU.add, op1=ALU.mult)
+            t_tiles[s] = (t, rstd)
+
+        def epi2(s, h):
+            n, m = divmod(s, 8)
+            t, rstd = t_tiles[s]
+            if h == 0:
+                cy_tiles[s] = epi.tile([P, D], F32, name="cy", tag="cy", bufs=4)
+            cy = cy_tiles[s]
+            cols = slice(HALF * h, HALF * (h + 1))
+            nc.vector.scalar_tensor_tensor(out=cy[:, cols], in0=t[:, cols], scalar=rstd, in1=c_tiles[(s, h)][:], op0=ALU.mult, op1=ALU.add)
+            nc.sync.dma_start(out=out[n, P * m : P * (m + 1), cols], in_=cy[:, cols])
+
+        def load_gain_bias(n):
+            cols = slice(D * n, D * (n + 1))
+            nc.sync.dma_start(out=b_bc[:, cols], in_=pln_b[n, :].partition_broadcast(P))
+            nc.sync.dma_start(out=g_bc[:, cols], in_=pln_g[n, :].partition_broadcast(P))
+
+        def item(k):
+            load_pairs(k + LOAD_LEAD)
+            widen(k)
+            transp(k)
+            evac(k)
+
+        def late_quantise(k):
+            quantise("w", k - 2)
+            quantise("a", k - 3)
+
+        nc.sync.dma_start(out=scale_bc[:], in_=pt_w_scale.rearrange("a b k -> (a b k)").partition_broadcast(P))
+        nc.vector.memset(b_rows[:], 0.0)
+        nc.sync.dma_start(out=b_rows[0 : NB * 8, :], in_=pln_b.rearrange("n (j p) -> (n j) p", p=P))
+        load_pairs(0)
+        load_pairs(2)
+        make_identity(nc, ident[:])
+        make_identity(nc, ident_bf[:])
+        nc.vector.memset(one[:], 1.0)
+        nc.vector.memset(sel0[:], 0.0)
+        nc.vector.memset(sel0[0:1, :], 1.0)
+        nc.scalar.activation(out=warm[:], in_=one[:], func=ACT.Abs_reciprocal_sqrt)
+
+        for k in range(ITEM_LEAD):
+            item(k)
+            late_quantise(k)
+            if k == 1:
+                bt = tps.tile([P, P], BF16, name="bt", tag="tp")
+                nc.tensor.transpose(bt[:], b_rows[:], ident_bf[:])
+                nc.scalar.copy(out=b_col[:], in_=bt[:, 0 : NB * 8])
+            if k == 6:
+                load_gain_bias(0)
+                for s in range(4):
+                    load_pw(s)
+            if k == 9:
+                mx(0)
+                stats(0)
+            if k == 10:
+                mx(1)
+                stats(1)
+                c_pe(0)
+                c_g(0)
+
+        for s in range(N_STEPS):
+            k = s + ITEM_LEAD
+            load_pw(s + 4)
+            load_pairs(k + LOAD_LEAD)
+            if s % 8 == 0 and s // 8 + 1 < NB:
+                load_gain_bias(s // 8 + 1)
+            epi1(s)
+            mx(s + 2)
+            stats(s + 2)
+            c_pe(s + 1)
+            widen(k)
+            transp(k)
+            evac(k)
+            late_quantise(k)
+            epi2(s, 0)
+            c_g(s + 1)
+            epi2(s, 1)

@@ -37,7 +37,7 @@ def tile_moietransformerblock_pb_kernel(tc, in_proto, pt_w_bytes, pt_w_scale, pl
         small = ctx.enter_context(tc.tile_pool(name="small", bufs=6))
         tps = ctx.enter_context(tc.psum_pool(name="tps", bufs=2))
         cps = ctx.enter_context(tc.psum_pool(name="cps", bufs=2))
-        xps = ctx.enter_context(tc.psum_pool(name="xps", bufs=2))
+        xps = ctx.enter_context(tc.psum_pool(name="xps", bufs=4))
         ctx.enter_context(tc.manual_schedule())
 
         scale_bc = const.tile([P, K], F32, name="scale_bc")
@@ -95,12 +95,12 @@ def tile_moietransformerblock_pb_kernel(tc, in_proto, pt_w_bytes, pt_w_scale, pl
                         nc.tensor.transpose(tp[:, g, u, :], words[:, 256 * g + u : 256 * (g + 1) : 2], ident[:])
                 tp_tiles[(op, k)] = tp
 
-        def evac(k):
+        def evac(k, ops=("a", "w")):
             if k >= N_ITEMS:
                 return
             n, i = divmod(k, 8)
             h, ii = divmod(i, 4)
-            for op in ("a", "w"):
+            for op in ops:
                 if ii == 0:
                     grouped[(op, n, h)] = work.tile([P, 2 * 2048], BF16, name="grouped", tag="grouped", bufs=4, align_bytes=64)
                 grp = grouped[(op, n, h)]
@@ -127,54 +127,77 @@ def tile_moietransformerblock_pb_kernel(tc, in_proto, pt_w_bytes, pt_w_scale, pl
             nc.sync.dma_start(out=t[:], in_=proto_w[n, P * m : P * (m + 1), :])
             pw_tiles[s] = t
 
-        def mx(s):
+        def mx(s, h):
             if s >= N_STEPS:
                 return
             n, m = divmod(s, 8)
             hf, mm = divmod(m, 4)
             a_cd, a_sc = codes[("a", n, hf)]
-            x = xps.tile([P, D], F32, name="x", tag="x")
-            for h in range(2):
-                w_cd, w_sc = codes[("w", n, h)]
-                for g in range(2):
-                    a_cols = slice(HALF * g + P * mm, HALF * g + P * (mm + 1))
-                    w_cols = slice(HALF * g, HALF * (g + 1))
-                    nc.tensor.matmul_mx(
-                        out=x[:, HALF * h : HALF * (h + 1)],
-                        lhsT=a_cd[:, a_cols].bitcast(FP8X4),
-                        lhsT_scale=a_sc[:, a_cols],
-                        rhs=w_cd[:, w_cols].bitcast(FP8X4),
-                        rhs_scale=w_sc[:, w_cols],
-                        start=(g == 0),
-                        stop=(g == 1),
-                    )
-            x_tiles[s] = x
+            w_cd, w_sc = codes[("w", n, h)]
+            x = xps.tile([P, HALF], F32, name="x", tag="x")
+            for g in range(2):
+                a_cols = slice(HALF * g + P * mm, HALF * g + P * (mm + 1))
+                w_cols = slice(HALF * g, HALF * (g + 1))
+                nc.tensor.matmul_mx(
+                    out=x[:],
+                    lhsT=a_cd[:, a_cols].bitcast(FP8X4),
+                    lhsT_scale=a_sc[:, a_cols],
+                    rhs=w_cd[:, w_cols].bitcast(FP8X4),
+                    rhs_scale=w_sc[:, w_cols],
+                    start=(g == 0),
+                    stop=(g == 1),
+                )
+            x_tiles[(s, h)] = x
 
-        def stats(t):
-            def pass_over(h, func, scale, bias, col):
-                if t < N_STEPS:
-                    junk = work.tile([P, HALF], BF16, name="junk", tag="junk")
-                    nc.scalar.activation(out=junk[:], in_=x_tiles[t][:, HALF * h : HALF * (h + 1)], func=func, scale=scale, bias=bias, accum_out=sum_tiles[t][:, col : col + 1])
+        def live(t):
+            return 0 <= t < N_STEPS
 
-            if t < N_STEPS:
+        def pass_over(t, h, func, scale, bias, col):
+            junk = work.tile([P, HALF], BF16, name="junk", tag="junk")
+            nc.scalar.activation(out=junk[:], in_=x_tiles[(t, h)][:], func=func, scale=scale, bias=bias, accum_out=sum_tiles[t][:, col : col + 1])
+
+        def sum_pass(t, h):
+            if not live(t):
+                return
+            if h == 0:
                 sum_tiles[t] = small.tile([P, 4], F32, name="sums", tag="sums")
                 stat_tiles[t] = small.tile([P, 6], F32, name="stat", tag="stat")
+            pass_over(t, h, ACT.Copy, HALF_MEAN_SCALE, 0.0, h)
+
+        def sq_pass(t, h):
+            if live(t):
+                pass_over(t, h, ACT.Square, 1.0 / 32, sum_tiles[t][:, h : h + 1], 2 + h)
+
+        def join0(t):
+            if live(t):
+                nc.scalar.activation(out=stat_tiles[t][:, 0:1], in_=sum_tiles[t][:, 1:2], func=ACT.Copy, scale=16.0)
+
+        def join12(t):
+            if live(t):
                 sums, stat = sum_tiles[t], stat_tiles[t]
-            if 0 <= t - 1 < N_STEPS:
-                psums, pstat = sum_tiles[t - 1], stat_tiles[t - 1]
-            pass_over(0, ACT.Copy, HALF_MEAN_SCALE, 0.0, 0)
-            if 0 <= t - 1 < N_STEPS:
-                nc.scalar.activation(out=pstat[:, 3:4], in_=psums[:, 3:4], func=ACT.Copy, scale=1.0, bias=LN_EPS)
-                nc.scalar.activation(out=pstat[:, 4:5], in_=psums[:, 2:3], func=ACT.Identity, bias=pstat[:, 2:3])
-            pass_over(1, ACT.Copy, HALF_MEAN_SCALE, 0.0, 1)
-            if 0 <= t - 1 < N_STEPS:
-                nc.scalar.activation(out=pstat[:, 5:6], in_=pstat[:, 3:4], func=ACT.Abs_reciprocal_sqrt, bias=pstat[:, 4:5])
-            if t < N_STEPS:
-                pass_over(0, ACT.Square, 1.0 / 32, sums[:, 0:1], 2)
-                nc.scalar.activation(out=stat[:, 0:1], in_=sums[:, 1:2], func=ACT.Copy, scale=16.0)
-                pass_over(1, ACT.Square, 1.0 / 32, sums[:, 1:2], 3)
                 nc.scalar.activation(out=stat[:, 1:2], in_=sums[:, 0:1], func=ACT.Identity, scale=16.0, bias=stat[:, 0:1])
                 nc.scalar.activation(out=stat[:, 2:3], in_=sums[:, 0:1], func=ACT.Square, scale=-16.0, bias=stat[:, 0:1])
+
+        def fin1(t):
+            if live(t):
+                sums, stat = sum_tiles[t], stat_tiles[t]
+                nc.scalar.activation(out=stat[:, 3:4], in_=sums[:, 3:4], func=ACT.Copy, scale=1.0, bias=LN_EPS)
+                nc.scalar.activation(out=stat[:, 4:5], in_=sums[:, 2:3], func=ACT.Identity, bias=stat[:, 2:3])
+
+        def fin2(t):
+            if live(t):
+                stat = stat_tiles[t]
+                nc.scalar.activation(out=stat[:, 5:6], in_=stat[:, 3:4], func=ACT.Abs_reciprocal_sqrt, bias=stat[:, 4:5])
+
+        def stats(t):
+            sum_pass(t, 0)
+            fin1(t - 1)
+            sum_pass(t, 1)
+            fin2(t - 1)
+            sq_pass(t, 0)
+            join0(t)
+            sq_pass(t, 1)
+            join12(t)
 
         def c_pe(s):
             if s >= N_STEPS:
@@ -207,13 +230,12 @@ def tile_moietransformerblock_pb_kernel(tc, in_proto, pt_w_bytes, pt_w_scale, pl
 
         def epi1(s):
             n = s // 8
-            x = x_tiles[s]
             stat = stat_tiles[s]
             rstd = stat[:, 5:6]
             t = epi.tile([P, D], F32, name="t", tag="t")
             for h in range(2):
                 cols = slice(HALF * h, HALF * (h + 1))
-                nc.vector.scalar_tensor_tensor(out=t[:, cols], in0=x[:, cols], scalar=stat[:, 1:2], in1=g_bc[:, D * n + HALF * h : D * n + HALF * (h + 1)], op0=ALU.add, op1=ALU.mult)
+                nc.vector.scalar_tensor_tensor(out=t[:, cols], in0=x_tiles[(s, h)][:], scalar=stat[:, 1:2], in1=g_bc[:, D * n + HALF * h : D * n + HALF * (h + 1)], op0=ALU.add, op1=ALU.mult)
             t_tiles[s] = (t, rstd)
 
         def epi2(s, h):
@@ -265,10 +287,12 @@ def tile_moietransformerblock_pb_kernel(tc, in_proto, pt_w_bytes, pt_w_scale, pl
                 for s in range(4):
                     load_pw(s)
             if k == 9:
-                mx(0)
+                mx(0, 0)
+                mx(0, 1)
                 stats(0)
             if k == 10:
-                mx(1)
+                mx(1, 0)
+                mx(1, 1)
                 stats(1)
                 c_pe(0)
                 c_g(0)
@@ -280,12 +304,27 @@ def tile_moietransformerblock_pb_kernel(tc, in_proto, pt_w_bytes, pt_w_scale, pl
             if s % 8 == 0 and s // 8 + 1 < NB:
                 load_gain_bias(s // 8 + 1)
             epi1(s)
-            mx(s + 2)
-            stats(s + 2)
+            if k < N_ITEMS:
+                mx(s + 2, 0)
+                sum_pass(s + 2, 0)
+                fin1(s + 1)
+                widen(k)
+                transp(k, ("a",))
+                evac(k, ("a",))
+                sq_pass(s + 2, 0)
+                fin2(s + 1)
+                mx(s + 2, 1)
+                sum_pass(s + 2, 1)
+                transp(k, ("w",))
+                evac(k, ("w",))
+                join0(s + 2)
+                sq_pass(s + 2, 1)
+                join12(s + 2)
+            else:
+                mx(s + 2, 0)
+                mx(s + 2, 1)
+                stats(s + 2)
             c_pe(s + 1)
-            widen(k)
-            transp(k)
-            evac(k)
             late_quantise(k)
             epi2(s, 0)
             c_g(s + 1)

@@ -20,7 +20,9 @@ P = 128
 HALF = 512
 N_STEPS = NB * 8
 N_ITEMS = NB * 8
-LATE = 12
+LATE = 8
+WARM_START = 4
+WARM_ITEMS = 9
 HALF_MEAN_SCALE = -1.0 / (32 * HALF)
 ITEM_LEAD = 12
 LOAD_LEAD = 4
@@ -253,10 +255,18 @@ def tile_moietransformerblock_pb_kernel(tc, in_proto, pt_w_bytes, pt_w_scale, pl
             nc.sync.dma_start(out=b_bc[:, cols], in_=pln_b[n, :].partition_broadcast(P))
             nc.sync.dma_start(out=g_bc[:, cols], in_=pln_g[n, :].partition_broadcast(P))
 
+        def keep_warm(count):
+            for i in range(count):
+                wd = xps.tile([P, P], F32, name="warm_ps", tag="x")
+                nc.tensor.matmul(out=wd[:], lhsT=ident[:], rhs=ident[:], start=True, stop=True)
+
         def item(k):
             load_pairs(k + LOAD_LEAD)
             widen(k)
-            transp(k)
+            for op in ("a", "w"):
+                transp(k, (op,))
+                if k < WARM_ITEMS:
+                    keep_warm(1)
             evac(k)
 
         def late_quantise(k):
@@ -274,6 +284,7 @@ def tile_moietransformerblock_pb_kernel(tc, in_proto, pt_w_bytes, pt_w_scale, pl
         nc.vector.memset(sel0[:], 0.0)
         nc.vector.memset(sel0[0:1, :], 1.0)
         nc.scalar.activation(out=warm[:], in_=one[:], func=ACT.Abs_reciprocal_sqrt)
+        keep_warm(WARM_START)
 
         for k in range(ITEM_LEAD):
             item(k)

@@ -20,10 +20,9 @@ P = 128
 HALF = 512
 N_STEPS = NB * 8
 N_ITEMS = NB * 8
-LATE = 8
-WARM_START = 4
+LATE = 6
+WARM_START = 12
 WARM_ITEMS = 9
-HALF_MEAN_SCALE = -1.0 / (32 * HALF)
 ITEM_LEAD = 12
 LOAD_LEAD = 4
 
@@ -163,43 +162,42 @@ def tile_moietransformerblock_pb_kernel(tc, in_proto, pt_w_bytes, pt_w_scale, pl
                 return
             if h == 0:
                 sum_tiles[t] = small.tile([P, 4], F32, name="sums", tag="sums")
-                stat_tiles[t] = small.tile([P, 6], F32, name="stat", tag="stat")
-            pass_over(t, h, ACT.Copy, HALF_MEAN_SCALE, 0.0, h)
+                stat_tiles[t] = small.tile([P, 5], F32, name="stat", tag="stat")
+            pass_over(t, h, ACT.Copy, -1.0 / D, 0.0, h)
 
         def sq_pass(t, h):
             if live(t):
-                pass_over(t, h, ACT.Square, 1.0 / 32, sum_tiles[t][:, h : h + 1], 2 + h)
+                pass_over(t, h, ACT.Square, 0.5, sum_tiles[t][:, h : h + 1], 2 + h)
 
-        def join0(t):
-            if live(t):
-                nc.scalar.activation(out=stat_tiles[t][:, 0:1], in_=sum_tiles[t][:, 1:2], func=ACT.Copy, scale=16.0)
-
-        def join12(t):
+        def means(t):
             if live(t):
                 sums, stat = sum_tiles[t], stat_tiles[t]
-                nc.scalar.activation(out=stat[:, 1:2], in_=sums[:, 0:1], func=ACT.Identity, scale=16.0, bias=stat[:, 0:1])
-                nc.scalar.activation(out=stat[:, 2:3], in_=sums[:, 0:1], func=ACT.Square, scale=-16.0, bias=stat[:, 0:1])
+                nc.scalar.activation(out=stat[:, 0:1], in_=sums[:, 0:1], func=ACT.Identity, bias=sums[:, 1:2])
+                nc.scalar.activation(out=stat[:, 1:2], in_=sums[:, 0:1], func=ACT.Square, scale=-1.0, bias=sums[:, 1:2])
 
-        def fin1(t):
+        def var_a(t):
             if live(t):
-                sums, stat = sum_tiles[t], stat_tiles[t]
-                nc.scalar.activation(out=stat[:, 3:4], in_=sums[:, 3:4], func=ACT.Copy, scale=1.0, bias=LN_EPS)
-                nc.scalar.activation(out=stat[:, 4:5], in_=sums[:, 2:3], func=ACT.Identity, bias=stat[:, 2:3])
+                nc.scalar.activation(out=stat_tiles[t][:, 2:3], in_=sum_tiles[t][:, 2:3], func=ACT.Copy, scale=1.0 / 256, bias=LN_EPS)
 
-        def fin2(t):
+        def var_b(t):
             if live(t):
                 stat = stat_tiles[t]
-                nc.scalar.activation(out=stat[:, 5:6], in_=stat[:, 3:4], func=ACT.Abs_reciprocal_sqrt, bias=stat[:, 4:5])
+                nc.scalar.activation(out=stat[:, 3:4], in_=stat[:, 1:2], func=ACT.Identity, bias=stat[:, 2:3])
 
-        def stats(t):
-            sum_pass(t, 0)
-            fin1(t - 1)
-            sum_pass(t, 1)
-            fin2(t - 1)
-            sq_pass(t, 0)
-            join0(t)
-            sq_pass(t, 1)
-            join12(t)
+        def r_std(t):
+            if live(t):
+                stat = stat_tiles[t]
+                nc.scalar.activation(out=stat[:, 4:5], in_=sum_tiles[t][:, 3:4], func=ACT.Abs_reciprocal_sqrt, scale=1.0 / 256, bias=stat[:, 3:4])
+
+        def stats(s):
+            sq_pass(s + 1, 0)
+            means(s + 1)
+            sq_pass(s + 1, 1)
+            var_a(s + 1)
+            sum_pass(s + 2, 0)
+            var_b(s + 1)
+            sum_pass(s + 2, 1)
+            r_std(s + 1)
 
         def c_pe(s):
             if s >= N_STEPS:
@@ -233,11 +231,11 @@ def tile_moietransformerblock_pb_kernel(tc, in_proto, pt_w_bytes, pt_w_scale, pl
         def epi1(s):
             n = s // 8
             stat = stat_tiles[s]
-            rstd = stat[:, 5:6]
+            rstd = stat[:, 4:5]
             t = epi.tile([P, D], F32, name="t", tag="t")
             for h in range(2):
                 cols = slice(HALF * h, HALF * (h + 1))
-                nc.vector.scalar_tensor_tensor(out=t[:, cols], in0=x_tiles[(s, h)][:], scalar=stat[:, 1:2], in1=g_bc[:, D * n + HALF * h : D * n + HALF * (h + 1)], op0=ALU.add, op1=ALU.mult)
+                nc.vector.scalar_tensor_tensor(out=t[:, cols], in0=x_tiles[(s, h)][:], scalar=stat[:, 0:1], in1=g_bc[:, D * n + HALF * h : D * n + HALF * (h + 1)], op0=ALU.add, op1=ALU.mult)
             t_tiles[s] = (t, rstd)
 
         def epi2(s, h):
@@ -246,9 +244,12 @@ def tile_moietransformerblock_pb_kernel(tc, in_proto, pt_w_bytes, pt_w_scale, pl
             if h == 0:
                 cy_tiles[s] = epi.tile([P, D], F32, name="cy", tag="cy", bufs=4)
             cy = cy_tiles[s]
-            cols = slice(HALF * h, HALF * (h + 1))
-            nc.vector.scalar_tensor_tensor(out=cy[:, cols], in0=t[:, cols], scalar=rstd, in1=c_tiles[(s, h)][:], op0=ALU.mult, op1=ALU.add)
-            nc.sync.dma_start(out=out[n, P * m : P * (m + 1), cols], in_=cy[:, cols])
+            pieces = 2 if (s == N_STEPS - 1 and h == 1) else 1
+            width = HALF // pieces
+            for q in range(pieces):
+                cols = slice(HALF * h + width * q, HALF * h + width * (q + 1))
+                nc.vector.scalar_tensor_tensor(out=cy[:, cols], in0=t[:, cols], scalar=rstd, in1=c_tiles[(s, h)][:, width * q : width * (q + 1)], op0=ALU.mult, op1=ALU.add)
+                nc.sync.dma_start(out=out[n, P * m : P * (m + 1), cols], in_=cy[:, cols])
 
         def load_gain_bias(n):
             cols = slice(D * n, D * (n + 1))
@@ -300,11 +301,11 @@ def tile_moietransformerblock_pb_kernel(tc, in_proto, pt_w_bytes, pt_w_scale, pl
             if k == 9:
                 mx(0, 0)
                 mx(0, 1)
-                stats(0)
+                stats(-2)
             if k == 10:
                 mx(1, 0)
                 mx(1, 1)
-                stats(1)
+                stats(-1)
                 c_pe(0)
                 c_g(0)
 
@@ -316,25 +317,25 @@ def tile_moietransformerblock_pb_kernel(tc, in_proto, pt_w_bytes, pt_w_scale, pl
                 load_gain_bias(s // 8 + 1)
             epi1(s)
             if k < N_ITEMS:
+                sq_pass(s + 1, 0)
+                means(s + 1)
+                sq_pass(s + 1, 1)
+                var_a(s + 1)
                 mx(s + 2, 0)
                 sum_pass(s + 2, 0)
-                fin1(s + 1)
+                var_b(s + 1)
                 widen(k)
                 transp(k, ("a",))
                 evac(k, ("a",))
-                sq_pass(s + 2, 0)
-                fin2(s + 1)
                 mx(s + 2, 1)
                 sum_pass(s + 2, 1)
+                r_std(s + 1)
                 transp(k, ("w",))
                 evac(k, ("w",))
-                join0(s + 2)
-                sq_pass(s + 2, 1)
-                join12(s + 2)
             else:
                 mx(s + 2, 0)
                 mx(s + 2, 1)
-                stats(s + 2)
+                stats(s)
             c_pe(s + 1)
             late_quantise(k)
             epi2(s, 0)

@@ -99,26 +99,24 @@ def tile_moietransformerblock_pb_kernel(tc, in_proto, pt_w_bytes, pt_w_scale, pl
         def evac(k, ops=("a", "w")):
             if k >= N_ITEMS:
                 return
-            n, i = divmod(k, 8)
-            h, ii = divmod(i, 4)
+            j, ii = divmod(k, 2)
             for op in ops:
                 if ii == 0:
-                    grouped[(op, n, h)] = work.tile([P, 2 * 2048], BF16, name="grouped", tag="grouped", bufs=4, align_bytes=64)
-                grp = grouped[(op, n, h)]
+                    grouped[(op, j)] = work.tile([P, 2048], BF16, name="grouped", tag="grouped", bufs=6, align_bytes=64)
+                grp = grouped[(op, j)]
                 nc.scalar.copy(
                     out=grp[:].bitcast(F32).rearrange("p (g r u) -> p g r u", g=2, u=2)[:, :, P * ii : P * (ii + 1), :],
                     in_=tp_tiles[(op, k)][:].rearrange("p g u r -> p g r u"),
                 )
 
         def quantise(op, k):
-            if k < 0 or k >= N_ITEMS or k % 4 != 3:
+            if k < 0 or k >= N_ITEMS or k % 2 != 1:
                 return
-            n, i = divmod(k, 8)
-            h = i // 4
-            cd = quant.tile([P, 1024], U32, name=op + "_codes", tag=op + "_codes", align_bytes=64)
-            sc = quant.tile([P, 1024], U8, name=op + "_scales", tag=op + "_scales", align_bytes=64)
-            nc.vector.quantize_mx(out=cd[:].bitcast(FP8X4), scales=sc[:], in_=grouped[(op, n, h)][:])
-            codes[(op, n, h)] = (cd, sc)
+            depth = 8 if op == "w" else 4
+            cd = quant.tile([P, HALF], U32, name=op + "_codes", tag=op + "_codes", bufs=depth, align_bytes=64)
+            sc = quant.tile([P, HALF], U8, name=op + "_scales", tag=op + "_scales", bufs=depth, align_bytes=64)
+            nc.vector.quantize_mx(out=cd[:].bitcast(FP8X4), scales=sc[:], in_=grouped[(op, k // 2)][:])
+            codes[(op, k // 2)] = (cd, sc)
 
         def load_pw(s):
             if s >= N_STEPS:
@@ -131,23 +129,22 @@ def tile_moietransformerblock_pb_kernel(tc, in_proto, pt_w_bytes, pt_w_scale, pl
         def mx(s, h):
             if s >= N_STEPS:
                 return
-            n, m = divmod(s, 8)
-            hf, mm = divmod(m, 4)
-            a_cd, a_sc = codes[("a", n, hf)]
-            w_cd, w_sc = codes[("w", n, h)]
+            a_cd, a_sc = codes[("a", s // 2)]
             x = xps.tile([P, HALF], F32, name="x", tag="x")
-            for g in range(2):
-                a_cols = slice(HALF * g + P * mm, HALF * g + P * (mm + 1))
-                w_cols = slice(HALF * g, HALF * (g + 1))
-                nc.tensor.matmul_mx(
-                    out=x[:],
-                    lhsT=a_cd[:, a_cols].bitcast(FP8X4),
-                    lhsT_scale=a_sc[:, a_cols],
-                    rhs=w_cd[:, w_cols].bitcast(FP8X4),
-                    rhs_scale=w_sc[:, w_cols],
-                    start=(g == 0),
-                    stop=(g == 1),
-                )
+            for jj in range(2):
+                w_cd, w_sc = codes[("w", 4 * (s // 8) + 2 * h + jj)]
+                for g in range(2):
+                    a_cols = slice(256 * g + P * (s % 2), 256 * g + P * (s % 2 + 1))
+                    w_cols = slice(256 * g, 256 * (g + 1))
+                    nc.tensor.matmul_mx(
+                        out=x[:, 256 * jj : 256 * (jj + 1)],
+                        lhsT=a_cd[:, a_cols].bitcast(FP8X4),
+                        lhsT_scale=a_sc[:, a_cols],
+                        rhs=w_cd[:, w_cols].bitcast(FP8X4),
+                        rhs_scale=w_sc[:, w_cols],
+                        start=(g == 0),
+                        stop=(g == 1),
+                    )
             x_tiles[(s, h)] = x
 
         def live(t):

@@ -24,14 +24,16 @@ LATE = 6
 WARM_START = 12
 WARM_ITEMS = 9
 ITEM_LEAD = 12
-LOAD_LEAD = 4
+LOAD_LEAD = 6
+WIDE_LEAD = 2
+X_FREE_ITEMS = 9
 
 
 def tile_moietransformerblock_pb_kernel(tc, in_proto, pt_w_bytes, pt_w_scale, pln_g, pln_b, proto_w, out):
     nc = tc.nc
     with ExitStack() as ctx:
         const = ctx.enter_context(tc.tile_pool(name="const", bufs=1))
-        raw = ctx.enter_context(tc.tile_pool(name="raw", bufs=4))
+        raw = ctx.enter_context(tc.tile_pool(name="raw", bufs=5))
         work = ctx.enter_context(tc.tile_pool(name="work", bufs=3))
         quant = ctx.enter_context(tc.tile_pool(name="quant", bufs=4))
         epi = ctx.enter_context(tc.tile_pool(name="epi", bufs=3))
@@ -63,7 +65,6 @@ def tile_moietransformerblock_pb_kernel(tc, in_proto, pt_w_bytes, pt_w_scale, pl
         x_tiles = {}
         t_tiles = {}
         stat_tiles = {}
-        sum_tiles = {}
 
         def load_pairs(k):
             if k >= N_ITEMS or k % 2 == 1:
@@ -80,7 +81,7 @@ def tile_moietransformerblock_pb_kernel(tc, in_proto, pt_w_bytes, pt_w_scale, pl
         def widen(k):
             if k >= N_ITEMS:
                 return
-            wide = work.tile([P, K], BF16, name="w_wide", tag="w_wide")
+            wide = work.tile([P, K], BF16, name="w_wide", tag="w_wide", bufs=3 + WIDE_LEAD)
             nc.vector.tensor_tensor(out=wide[:], in0=raw_tiles[("w", k - k % 2)][:, k % 2, :].bitcast(FP8), in1=scale_bc[:], op=ALU.mult)
             wide_tiles[k] = wide
 
@@ -90,7 +91,10 @@ def tile_moietransformerblock_pb_kernel(tc, in_proto, pt_w_bytes, pt_w_scale, pl
             for op in ops:
                 src = wide_tiles[k][:] if op == "w" else raw_tiles[("a", k - k % 2)][:, k % 2, :]
                 words = src.bitcast(F32)
-                tp = tps.tile([P, 2, 2, P], F32, name="tp", tag="tp")
+                if op == "a" and k < X_FREE_ITEMS:
+                    tp = xps.tile([P, 2, 2, P], F32, name="tp_x", tag="x")
+                else:
+                    tp = tps.tile([P, 2, 2, P], F32, name="tp", tag="tp")
                 for g in range(2):
                     for u in range(2):
                         nc.tensor.transpose(tp[:, g, u, :], words[:, 256 * g + u : 256 * (g + 1) : 2], ident[:])
@@ -130,7 +134,10 @@ def tile_moietransformerblock_pb_kernel(tc, in_proto, pt_w_bytes, pt_w_scale, pl
             if s >= N_STEPS:
                 return
             a_cd, a_sc = codes[("a", s // 2)]
-            x = xps.tile([P, HALF], F32, name="x", tag="x")
+            if s >= N_ITEMS - ITEM_LEAD + 2 and (s - (N_ITEMS - ITEM_LEAD + 2)) % 3 == 0:
+                x = tps.tile([P, HALF], F32, name="x_tp", tag="tp")
+            else:
+                x = xps.tile([P, HALF], F32, name="x", tag="x")
             for jj in range(2):
                 w_cd, w_sc = codes[("w", 4 * (s // 8) + 2 * h + jj)]
                 for g in range(2):
@@ -152,47 +159,35 @@ def tile_moietransformerblock_pb_kernel(tc, in_proto, pt_w_bytes, pt_w_scale, pl
 
         def pass_over(t, h, func, scale, bias, col):
             junk = work.tile([P, HALF], BF16, name="junk", tag="junk")
-            nc.scalar.activation(out=junk[:], in_=x_tiles[(t, h)][:], func=func, scale=scale, bias=bias, accum_out=sum_tiles[t][:, col : col + 1])
+            nc.scalar.activation(out=junk[:], in_=x_tiles[(t, h)][:], func=func, scale=scale, bias=bias, accum_out=stat_tiles[t][:, col : col + 1])
 
         def sum_pass(t, h):
             if not live(t):
                 return
             if h == 0:
-                sum_tiles[t] = small.tile([P, 4], F32, name="sums", tag="sums")
-                stat_tiles[t] = small.tile([P, 5], F32, name="stat", tag="stat")
-            pass_over(t, h, ACT.Copy, -1.0 / D, 0.0, h)
+                stat_tiles[t] = small.tile([P, 6], F32, name="stat", tag="stat")
+                pass_over(t, h, ACT.Copy, -1.0 / (D * HALF), 0.0, 0)
+            else:
+                pass_over(t, h, ACT.Identity, -1.0 / D, stat_tiles[t][:, 0:1], 1)
 
         def sq_pass(t, h):
             if live(t):
-                pass_over(t, h, ACT.Square, 0.5, sum_tiles[t][:, h : h + 1], 2 + h)
+                pass_over(t, h, ACT.Square, 1.0, stat_tiles[t][:, 1:2], 2 + h)
 
-        def means(t):
+        def var_0(t):
             if live(t):
-                sums, stat = sum_tiles[t], stat_tiles[t]
-                nc.scalar.activation(out=stat[:, 0:1], in_=sums[:, 0:1], func=ACT.Identity, bias=sums[:, 1:2])
-                nc.scalar.activation(out=stat[:, 1:2], in_=sums[:, 0:1], func=ACT.Square, scale=-1.0, bias=sums[:, 1:2])
-
-        def var_a(t):
-            if live(t):
-                nc.scalar.activation(out=stat_tiles[t][:, 2:3], in_=sum_tiles[t][:, 2:3], func=ACT.Copy, scale=1.0 / 256, bias=LN_EPS)
-
-        def var_b(t):
-            if live(t):
-                stat = stat_tiles[t]
-                nc.scalar.activation(out=stat[:, 3:4], in_=stat[:, 1:2], func=ACT.Identity, bias=stat[:, 2:3])
+                nc.scalar.activation(out=stat_tiles[t][:, 4:5], in_=stat_tiles[t][:, 2:3], func=ACT.Copy, scale=1.0 / D, bias=LN_EPS)
 
         def r_std(t):
             if live(t):
                 stat = stat_tiles[t]
-                nc.scalar.activation(out=stat[:, 4:5], in_=sum_tiles[t][:, 3:4], func=ACT.Abs_reciprocal_sqrt, scale=1.0 / 256, bias=stat[:, 3:4])
+                nc.scalar.activation(out=stat[:, 5:6], in_=stat[:, 3:4], func=ACT.Abs_reciprocal_sqrt, scale=1.0 / D, bias=stat[:, 4:5])
 
         def stats(s):
             sq_pass(s + 1, 0)
-            means(s + 1)
             sq_pass(s + 1, 1)
-            var_a(s + 1)
             sum_pass(s + 2, 0)
-            var_b(s + 1)
+            var_0(s + 1)
             sum_pass(s + 2, 1)
             r_std(s + 1)
 
@@ -228,11 +223,11 @@ def tile_moietransformerblock_pb_kernel(tc, in_proto, pt_w_bytes, pt_w_scale, pl
         def epi1(s):
             n = s // 8
             stat = stat_tiles[s]
-            rstd = stat[:, 4:5]
+            rstd = stat[:, 5:6]
             t = epi.tile([P, D], F32, name="t", tag="t")
             for h in range(2):
                 cols = slice(HALF * h, HALF * (h + 1))
-                nc.vector.scalar_tensor_tensor(out=t[:, cols], in0=x_tiles[(s, h)][:], scalar=stat[:, 0:1], in1=g_bc[:, D * n + HALF * h : D * n + HALF * (h + 1)], op0=ALU.add, op1=ALU.mult)
+                nc.vector.scalar_tensor_tensor(out=t[:, cols], in0=x_tiles[(s, h)][:], scalar=stat[:, 1:2], in1=g_bc[:, D * n + HALF * h : D * n + HALF * (h + 1)], op0=ALU.add, op1=ALU.mult)
             t_tiles[s] = (t, rstd)
 
         def epi2(s, h):
@@ -255,12 +250,12 @@ def tile_moietransformerblock_pb_kernel(tc, in_proto, pt_w_bytes, pt_w_scale, pl
 
         def keep_warm(count):
             for i in range(count):
-                wd = xps.tile([P, P], F32, name="warm_ps", tag="x")
+                wd = cps.tile([P, P], F32, name="warm_ps", tag="c")
                 nc.tensor.matmul(out=wd[:], lhsT=ident[:], rhs=ident[:], start=True, stop=True)
 
         def item(k):
             load_pairs(k + LOAD_LEAD)
-            widen(k)
+            widen(k + WIDE_LEAD)
             for op in ("a", "w"):
                 transp(k, (op,))
                 if k < WARM_ITEMS:
@@ -268,7 +263,8 @@ def tile_moietransformerblock_pb_kernel(tc, in_proto, pt_w_bytes, pt_w_scale, pl
             evac(k)
 
         def late_quantise(k):
-            quantise("w", k - 2)
+            if k <= N_ITEMS:
+                quantise("w", k - (1 if k == N_ITEMS else 2))
             quantise("a", k - 3)
 
         nc.sync.dma_start(out=scale_bc[:], in_=pt_w_scale.rearrange("a b k -> (a b k)").partition_broadcast(P))
@@ -276,6 +272,7 @@ def tile_moietransformerblock_pb_kernel(tc, in_proto, pt_w_bytes, pt_w_scale, pl
         nc.sync.dma_start(out=b_rows[0 : NB * 8, :], in_=pln_b.rearrange("n (j p) -> (n j) p", p=P))
         load_pairs(0)
         load_pairs(2)
+        load_pairs(4)
         make_identity(nc, ident[:])
         make_identity(nc, ident_bf[:])
         nc.vector.memset(one[:], 1.0)
@@ -284,6 +281,8 @@ def tile_moietransformerblock_pb_kernel(tc, in_proto, pt_w_bytes, pt_w_scale, pl
         nc.scalar.activation(out=warm[:], in_=one[:], func=ACT.Abs_reciprocal_sqrt)
         keep_warm(WARM_START)
 
+        for k in range(WIDE_LEAD):
+            widen(k)
         for k in range(ITEM_LEAD):
             item(k)
             late_quantise(k)
@@ -315,25 +314,32 @@ def tile_moietransformerblock_pb_kernel(tc, in_proto, pt_w_bytes, pt_w_scale, pl
             epi1(s)
             if k < N_ITEMS:
                 sq_pass(s + 1, 0)
-                means(s + 1)
                 sq_pass(s + 1, 1)
-                var_a(s + 1)
                 mx(s + 2, 0)
                 sum_pass(s + 2, 0)
-                var_b(s + 1)
-                widen(k)
+                var_0(s + 1)
+                widen(k + WIDE_LEAD)
                 transp(k, ("a",))
                 evac(k, ("a",))
                 mx(s + 2, 1)
-                sum_pass(s + 2, 1)
                 r_std(s + 1)
+                sum_pass(s + 2, 1)
                 transp(k, ("w",))
                 evac(k, ("w",))
             else:
-                mx(s + 2, 0)
-                mx(s + 2, 1)
-                stats(s)
+                mx(s + 3, 0)
+                mx(s + 3, 1)
+                sum_pass(s + 2, 0)
+                if s > N_ITEMS - ITEM_LEAD:
+                    r_std(s)
+                sq_pass(s + 1, 0)
+                sum_pass(s + 2, 1)
+                var_0(s + 1)
+                sq_pass(s + 1, 1)
             c_pe(s + 1)
+            if k == N_ITEMS - 1:
+                mx(s + 3, 0)
+                mx(s + 3, 1)
             late_quantise(k)
             epi2(s, 0)
             c_g(s + 1)

@@ -21,7 +21,7 @@ HALF = 512
 N_STEPS = NB * 8
 N_ITEMS = NB * 8
 LATE = 6
-WARM_START = 12
+WARM_START = 6
 WARM_ITEMS = 9
 ITEM_LEAD = 12
 LOAD_LEAD = 6
@@ -70,11 +70,13 @@ def tile_moietransformerblock_pb_kernel(tc, in_proto, pt_w_bytes, pt_w_scale, pl
             if k >= N_ITEMS or k % 2 == 1:
                 return
             n, i = divmod(k, 8)
-            rows = slice(P * i, P * (i + 2))
             wt = raw.tile([P, 2, K], U8, name="w_bytes", tag="w_bytes")
-            nc.sync.dma_start(out=wt[:], in_=pt_w_bytes[n, rows, :].rearrange("(i p) k -> p i k", p=P))
             at = raw.tile([P, 2, K], BF16, name="a_raw", tag="a_raw")
-            nc.sync.dma_start(out=at[:], in_=in_proto[n, rows, :].rearrange("(i p) k -> p i k", p=P))
+            for first, count in ((0, 1), (1, 1)) if k == 0 else ((0, 2),):
+                rows = slice(P * (i + first), P * (i + first + count))
+                part = slice(first, first + count)
+                nc.sync.dma_start(out=wt[:, part, :], in_=pt_w_bytes[n, rows, :].rearrange("(i p) k -> p i k", p=P))
+                nc.sync.dma_start(out=at[:, part, :], in_=in_proto[n, rows, :].rearrange("(i p) k -> p i k", p=P))
             raw_tiles[("w", k)] = wt
             raw_tiles[("a", k)] = at
 
@@ -269,8 +271,8 @@ def tile_moietransformerblock_pb_kernel(tc, in_proto, pt_w_bytes, pt_w_scale, pl
 
         nc.sync.dma_start(out=scale_bc[:], in_=pt_w_scale.rearrange("a b k -> (a b k)").partition_broadcast(P))
         nc.vector.memset(b_rows[:], 0.0)
-        nc.sync.dma_start(out=b_rows[0 : NB * 8, :], in_=pln_b.rearrange("n (j p) -> (n j) p", p=P))
         load_pairs(0)
+        nc.sync.dma_start(out=b_rows[0 : NB * 8, :], in_=pln_b.rearrange("n (j p) -> (n j) p", p=P))
         load_pairs(2)
         load_pairs(4)
         make_identity(nc, ident[:])
@@ -340,7 +342,10 @@ def tile_moietransformerblock_pb_kernel(tc, in_proto, pt_w_bytes, pt_w_scale, pl
             if k == N_ITEMS - 1:
                 mx(s + 3, 0)
                 mx(s + 3, 1)
-            late_quantise(k)
+            if k != N_ITEMS:
+                late_quantise(k)
             epi2(s, 0)
             c_g(s + 1)
             epi2(s, 1)
+            if k == N_ITEMS:
+                late_quantise(k)

@@ -258,10 +258,9 @@ def tile_moietransformerblock_pb_kernel(tc, in_proto, pt_w_bytes, pt_w_scale, pl
         def item(k):
             load_pairs(k + LOAD_LEAD)
             widen(k + WIDE_LEAD)
-            for op in ("a", "w"):
-                transp(k, (op,))
-                if k < WARM_ITEMS:
-                    keep_warm(1)
+            transp(k)
+            if k < WARM_ITEMS:
+                keep_warm(2)
             evac(k)
 
         def late_quantise(k):

@@ -21,7 +21,7 @@ HALF = 512
 N_STEPS = NB * 8
 N_ITEMS = NB * 8
 LATE = 6
-WARM_START = 6
+WARM_START = 4
 WARM_ITEMS = 9
 ITEM_LEAD = 12
 LOAD_LEAD = 6
@@ -46,6 +46,7 @@ def tile_moietransformerblock_pb_kernel(tc, in_proto, pt_w_bytes, pt_w_scale, pl
         scale_bc = const.tile([P, K], F32, name="scale_bc")
         g_bc = const.tile([P, NB * D], BF16, name="g_bc")
         b_bc = const.tile([P, NB * D], BF16, name="b_bc")
+        s_cols = const.tile([P, 8], F32, name="s_cols")
         b_rows = const.tile([P, P], BF16, name="b_rows")
         b_col = const.tile([P, NB * 8], F32, name="b_col")
         ident = const.tile([P, P], F32, name="ident")
@@ -268,7 +269,7 @@ def tile_moietransformerblock_pb_kernel(tc, in_proto, pt_w_bytes, pt_w_scale, pl
                 quantise("w", k - (1 if k == N_ITEMS else 2))
             quantise("a", k - 3)
 
-        nc.sync.dma_start(out=scale_bc[:], in_=pt_w_scale.rearrange("a b k -> (a b k)").partition_broadcast(P))
+        nc.sync.dma_start(out=s_cols[:], in_=pt_w_scale.rearrange("a b (j i) -> (a b j) i", i=8))
         nc.vector.memset(b_rows[:], 0.0)
         load_pairs(0)
         nc.sync.dma_start(out=b_rows[0 : NB * 8, :], in_=pln_b.rearrange("n (j p) -> (n j) p", p=P))
@@ -281,6 +282,12 @@ def tile_moietransformerblock_pb_kernel(tc, in_proto, pt_w_bytes, pt_w_scale, pl
         nc.vector.memset(sel0[0:1, :], 1.0)
         nc.scalar.activation(out=warm[:], in_=one[:], func=ACT.Abs_reciprocal_sqrt)
         keep_warm(WARM_START)
+        for h in range(2):
+            sb = xps.tile([P, 4, P], F32, name="sb", tag="x")
+            for i in range(4):
+                nc.tensor.transpose(sb[:, i, :], s_cols[:, 4 * h + i : 4 * h + i + 1].to_broadcast([P, P]), ident[:])
+            copy = nc.scalar.copy if h == 0 else nc.vector.tensor_copy
+            copy(out=scale_bc[:].rearrange("p (j i) -> p j i", i=8)[:, :, 4 * h : 4 * h + 4], in_=sb[:].rearrange("p i j -> p j i"))
 
         for k in range(WIDE_LEAD):
             widen(k)

@@ -21,7 +21,7 @@ HALF = 512
 N_STEPS = NB * 8
 N_ITEMS = NB * 8
 LATE = 6
-WARM_START = 4
+WARM_START = 2
 WARM_ITEMS = 9
 ITEM_LEAD = 12
 LOAD_LEAD = 6
@@ -46,7 +46,7 @@ def tile_moietransformerblock_pb_kernel(tc, in_proto, pt_w_bytes, pt_w_scale, pl
         scale_bc = const.tile([P, K], F32, name="scale_bc")
         g_bc = const.tile([P, NB * D], BF16, name="g_bc")
         b_bc = const.tile([P, NB * D], BF16, name="b_bc")
-        s_cols = const.tile([P, 8], F32, name="s_cols")
+        s_cols = const.tile([P, 2, 4], F32, name="s_cols")
         b_rows = const.tile([P, P], BF16, name="b_rows")
         b_col = const.tile([P, NB * 8], F32, name="b_col")
         ident = const.tile([P, P], F32, name="ident")
@@ -85,7 +85,10 @@ def tile_moietransformerblock_pb_kernel(tc, in_proto, pt_w_bytes, pt_w_scale, pl
             if k >= N_ITEMS:
                 return
             wide = work.tile([P, K], BF16, name="w_wide", tag="w_wide", bufs=3 + WIDE_LEAD)
-            nc.vector.tensor_tensor(out=wide[:], in0=raw_tiles[("w", k - k % 2)][:, k % 2, :].bitcast(FP8), in1=scale_bc[:], op=ALU.mult)
+            pieces = 2 if k == 0 else 1
+            for q in range(pieces):
+                cols = slice(K // pieces * q, K // pieces * (q + 1))
+                nc.vector.tensor_tensor(out=wide[:, cols], in0=raw_tiles[("w", k - k % 2)][:, k % 2, cols].bitcast(FP8), in1=scale_bc[:, cols], op=ALU.mult)
             wide_tiles[k] = wide
 
         def transp(k, ops=("a", "w")):
@@ -259,7 +262,12 @@ def tile_moietransformerblock_pb_kernel(tc, in_proto, pt_w_bytes, pt_w_scale, pl
         def item(k):
             load_pairs(k + LOAD_LEAD)
             widen(k + WIDE_LEAD)
-            transp(k)
+            if k >= 2:
+                transp(k)
+            elif k == 0:
+                for op in ("a", "w"):
+                    transp(0, (op,))
+                    transp(1, (op,))
             if k < WARM_ITEMS:
                 keep_warm(2)
             evac(k)
@@ -269,7 +277,7 @@ def tile_moietransformerblock_pb_kernel(tc, in_proto, pt_w_bytes, pt_w_scale, pl
                 quantise("w", k - (1 if k == N_ITEMS else 2))
             quantise("a", k - 3)
 
-        nc.sync.dma_start(out=s_cols[:], in_=pt_w_scale.rearrange("a b (j i) -> (a b j) i", i=8))
+        nc.sync.dma_start(out=s_cols[:], in_=pt_w_scale.rearrange("a b (h j i) -> (a b j) h i", h=2, i=4))
         nc.vector.memset(b_rows[:], 0.0)
         load_pairs(0)
         nc.sync.dma_start(out=b_rows[0 : NB * 8, :], in_=pln_b.rearrange("n (j p) -> (n j) p", p=P))
@@ -285,9 +293,8 @@ def tile_moietransformerblock_pb_kernel(tc, in_proto, pt_w_bytes, pt_w_scale, pl
         for h in range(2):
             sb = xps.tile([P, 4, P], F32, name="sb", tag="x")
             for i in range(4):
-                nc.tensor.transpose(sb[:, i, :], s_cols[:, 4 * h + i : 4 * h + i + 1].to_broadcast([P, P]), ident[:])
-            copy = nc.scalar.copy if h == 0 else nc.vector.tensor_copy
-            copy(out=scale_bc[:].rearrange("p (j i) -> p j i", i=8)[:, :, 4 * h : 4 * h + 4], in_=sb[:].rearrange("p i j -> p j i"))
+                nc.tensor.transpose(sb[:, i, :], s_cols[:, h, i : i + 1].to_broadcast([P, P]), ident[:])
+            nc.scalar.copy(out=scale_bc[:, HALF * h : HALF * (h + 1)].rearrange("p (j i) -> p j i", i=4), in_=sb[:].rearrange("p i j -> p j i"))
 
         for k in range(WIDE_LEAD):
             widen(k)

@@ -27,6 +27,7 @@ ITEM_LEAD = 12
 LOAD_LEAD = 6
 WIDE_LEAD = 2
 X_FREE_ITEMS = 9
+TP_FREE = 2 * (N_ITEMS - ITEM_LEAD + 2) + 1
 
 
 def tile_moietransformerblock_pb_kernel(tc, in_proto, pt_w_bytes, pt_w_scale, pln_g, pln_b, proto_w, out):
@@ -39,8 +40,8 @@ def tile_moietransformerblock_pb_kernel(tc, in_proto, pt_w_bytes, pt_w_scale, pl
         epi = ctx.enter_context(tc.tile_pool(name="epi", bufs=3))
         small = ctx.enter_context(tc.tile_pool(name="small", bufs=6))
         tps = ctx.enter_context(tc.psum_pool(name="tps", bufs=2))
-        cps = ctx.enter_context(tc.psum_pool(name="cps", bufs=2))
-        xps = ctx.enter_context(tc.psum_pool(name="xps", bufs=4))
+        cps = ctx.enter_context(tc.psum_pool(name="cps", bufs=1))
+        xps = ctx.enter_context(tc.psum_pool(name="xps", bufs=5))
         ctx.enter_context(tc.manual_schedule())
 
         scale_bc = const.tile([P, K], F32, name="scale_bc")
@@ -136,11 +137,12 @@ def tile_moietransformerblock_pb_kernel(tc, in_proto, pt_w_bytes, pt_w_scale, pl
             nc.sync.dma_start(out=t[:], in_=proto_w[n, P * m : P * (m + 1), :])
             pw_tiles[s] = t
 
-        def mx(s, h):
+        def mx(j):
+            s, h = divmod(j, 2)
             if s >= N_STEPS:
                 return
             a_cd, a_sc = codes[("a", s // 2)]
-            if s >= N_ITEMS - ITEM_LEAD + 2 and (s - (N_ITEMS - ITEM_LEAD + 2)) % 3 == 0:
+            if j >= TP_FREE and (j - TP_FREE) % 7 < 2:
                 x = tps.tile([P, HALF], F32, name="x_tp", tag="tp")
             else:
                 x = xps.tile([P, HALF], F32, name="x", tag="x")
@@ -255,9 +257,9 @@ def tile_moietransformerblock_pb_kernel(tc, in_proto, pt_w_bytes, pt_w_scale, pl
             nc.sync.dma_start(out=g_bc[:, cols], in_=pln_g[n, :].partition_broadcast(P))
 
         def keep_warm(count):
+            wd = cps.tile([P, count, P], F32, name="warm_ps", tag="c")
             for i in range(count):
-                wd = cps.tile([P, P], F32, name="warm_ps", tag="c")
-                nc.tensor.matmul(out=wd[:], lhsT=ident[:], rhs=ident[:], start=True, stop=True)
+                nc.tensor.matmul(out=wd[:, i, :], lhsT=ident[:], rhs=ident[:], start=True, stop=True)
 
         def item(k):
             load_pairs(k + LOAD_LEAD)
@@ -301,7 +303,7 @@ def tile_moietransformerblock_pb_kernel(tc, in_proto, pt_w_bytes, pt_w_scale, pl
         for k in range(ITEM_LEAD):
             item(k)
             late_quantise(k)
-            if k == 1:
+            if k == 3:
                 bt = tps.tile([P, P], BF16, name="bt", tag="tp")
                 nc.tensor.transpose(bt[:], b_rows[:], ident_bf[:])
                 nc.scalar.copy(out=b_col[:], in_=bt[:, 0 : NB * 8])
@@ -310,15 +312,17 @@ def tile_moietransformerblock_pb_kernel(tc, in_proto, pt_w_bytes, pt_w_scale, pl
                 for s in range(4):
                     load_pw(s)
             if k == 9:
-                mx(0, 0)
-                mx(0, 1)
+                mx(0)
+                mx(1)
                 stats(-2)
             if k == 10:
-                mx(1, 0)
-                mx(1, 1)
+                mx(2)
+                mx(3)
                 stats(-1)
                 c_pe(0)
                 c_g(0)
+            if k == 11:
+                mx(4)
 
         for s in range(N_STEPS):
             k = s + ITEM_LEAD
@@ -330,20 +334,20 @@ def tile_moietransformerblock_pb_kernel(tc, in_proto, pt_w_bytes, pt_w_scale, pl
             if k < N_ITEMS:
                 sq_pass(s + 1, 0)
                 sq_pass(s + 1, 1)
-                mx(s + 2, 0)
+                mx(2 * s + 5)
                 sum_pass(s + 2, 0)
                 var_0(s + 1)
                 widen(k + WIDE_LEAD)
                 transp(k, ("a",))
                 evac(k, ("a",))
-                mx(s + 2, 1)
+                mx(2 * s + 6)
                 r_std(s + 1)
                 sum_pass(s + 2, 1)
                 transp(k, ("w",))
                 evac(k, ("w",))
             else:
-                mx(s + 3, 0)
-                mx(s + 3, 1)
+                mx(2 * s + 7)
+                mx(2 * s + 8)
                 sum_pass(s + 2, 0)
                 if s > N_ITEMS - ITEM_LEAD:
                     r_std(s)
@@ -353,8 +357,8 @@ def tile_moietransformerblock_pb_kernel(tc, in_proto, pt_w_bytes, pt_w_scale, pl
                 sq_pass(s + 1, 1)
             c_pe(s + 1)
             if k == N_ITEMS - 1:
-                mx(s + 3, 0)
-                mx(s + 3, 1)
+                mx(2 * s + 7)
+                mx(2 * s + 8)
             if k != N_ITEMS:
                 late_quantise(k)
             epi2(s, 0)

from contextlib import ExitStack

import concourse.mybir as mybir
from concourse.masks import make_identity

NB, F, D, K = 3, 1024, 1024, 1024
FLOPS = 2 * NB * F * D * K
LN_EPS = 1e-5

F32 = mybir.dt.float32
BF16 = mybir.dt.bfloat16
U32 = mybir.dt.uint32
U8 = mybir.dt.uint8
FP8 = mybir.dt.float8_e4m3fn
FP8X4 = mybir.dt.float8_e4m3fn_x4
ALU = mybir.AluOpType
ACT = mybir.ActivationFunctionType

P = 128
HALF = 512
N_STEPS = NB * 8
N_ITEMS = NB * 8
LATE = 6
WARM_START = 2
WARM_ITEMS = 9
ITEM_LEAD = 12
LOAD_LEAD = 6
WIDE_LEAD = 2
X_FREE_ITEMS = 9
TP_FREE = 2 * (N_ITEMS - ITEM_LEAD + 2) + 1


def tile_moietransformerblock_pb_kernel(tc, in_proto, pt_w_bytes, pt_w_scale, pln_g, pln_b, proto_w, out):
    nc = tc.nc
    with ExitStack() as ctx:
        const = ctx.enter_context(tc.tile_pool(name="const", bufs=1))
        raw = ctx.enter_context(tc.tile_pool(name="raw", bufs=5))
        work = ctx.enter_context(tc.tile_pool(name="work", bufs=3))
        quant = ctx.enter_context(tc.tile_pool(name="quant", bufs=4))
        epi = ctx.enter_context(tc.tile_pool(name="epi", bufs=3))
        small = ctx.enter_context(tc.tile_pool(name="small", bufs=6))
        tps = ctx.enter_context(tc.psum_pool(name="tps", bufs=2))
        cps = ctx.enter_context(tc.psum_pool(name="cps", bufs=1))
        xps = ctx.enter_context(tc.psum_pool(name="xps", bufs=5))
        ctx.enter_context(tc.manual_schedule())

        scale_bc = const.tile([P, K], F32, name="scale_bc")
        g_bc = const.tile([P, NB * D], BF16, name="g_bc")
        b_bc = const.tile([P, NB * D], BF16, name="b_bc")
        s_cols = const.tile([P, 2, 4], F32, name="s_cols")
        b_rows = const.tile([P, P], BF16, name="b_rows")
        b_col = const.tile([P, NB * 8], F32, name="b_col")
        ident = const.tile([P, P], F32, name="ident")
        ident_bf = const.tile([P, P], BF16, name="ident_bf")
        sel0 = const.tile([P, P], BF16, name="sel0")
        one = const.tile([P, 1], F32, name="one")
        warm = const.tile([P, 1], F32, name="warm")

        raw_tiles = {}
        wide_tiles = {}
        tp_tiles = {}
        grouped = {}
        codes = {}
        pw_tiles = {}
        cy_tiles = {}
        c_tiles = {}
        x_tiles = {}
        t_tiles = {}
        stat_tiles = {}

        def load_pairs(k):
            if k >= N_ITEMS or k % 2 == 1:
                return
            n, i = divmod(k, 8)
            wt = raw.tile([P, 2, K], U8, name="w_bytes", tag="w_bytes")
            at = raw.tile([P, 2, K], BF16, name="a_raw", tag="a_raw")
            for first, count in ((0, 1), (1, 1)) if k == 0 else ((0, 2),):
                rows = slice(P * (i + first), P * (i + first + count))
                part = slice(first, first + count)
                nc.sync.dma_start(out=wt[:, part, :], in_=pt_w_bytes[n, rows, :].rearrange("(i p) k -> p i k", p=P))
                nc.sync.dma_start(out=at[:, part, :], in_=in_proto[n, rows, :].rearrange("(i p) k -> p i k", p=P))
            raw_tiles[("w", k)] = wt
            raw_tiles[("a", k)] = at

        def widen(k):
            if k >= N_ITEMS:
                return
            wide = work.tile([P, K], BF16, name="w_wide", tag="w_wide", bufs=3 + WIDE_LEAD)
            pieces = 2 if k == 0 else 1
            for q in range(pieces):
                cols = slice(K // pieces * q, K // pieces * (q + 1))
                nc.vector.tensor_tensor(out=wide[:, cols], in0=raw_tiles[("w", k - k % 2)][:, k % 2, cols].bitcast(FP8), in1=scale_bc[:, cols], op=ALU.mult)
            wide_tiles[k] = wide

        def transp(k, ops=("a", "w")):
            if k >= N_ITEMS:
                return
            for op in ops:
                src = wide_tiles[k][:] if op == "w" else raw_tiles[("a", k - k % 2)][:, k % 2, :]
                words = src.bitcast(F32)
                if op == "a" and k < X_FREE_ITEMS:
                    tp = xps.tile([P, 2, 2, P], F32, name="tp_x", tag="x")
                else:
                    tp = tps.tile([P, 2, 2, P], F32, name="tp", tag="tp")
                for g in range(2):
                    for u in range(2):
                        nc.tensor.transpose(tp[:, g, u, :], words[:, 256 * g + u : 256 * (g + 1) : 2], ident[:])
                tp_tiles[(op, k)] = tp

        def evac(k, ops=("a", "w")):
            if k >= N_ITEMS:
                return
            j, ii = divmod(k, 2)
            for op in ops:
                if ii == 0:
                    grouped[(op, j)] = work.tile([P, 2048], BF16, name="grouped", tag="grouped", bufs=6, align_bytes=64)
                grp = grouped[(op, j)]
                nc.scalar.copy(
                    out=grp[:].bitcast(F32).rearrange("p (g r u) -> p g r u", g=2, u=2)[:, :, P * ii : P * (ii + 1), :],
                    in_=tp_tiles[(op, k)][:].rearrange("p g u r -> p g r u"),
                )

        def quantise(op, k):
            if k < 0 or k >= N_ITEMS or k % 2 != 1:
                return
            depth = 8 if op == "w" else 4
            cd = quant.tile([P, HALF], U32, name=op + "_codes", tag=op + "_codes", bufs=depth, align_bytes=64)
            sc = quant.tile([P, HALF], U8, name=op + "_scales", tag=op + "_scales", bufs=depth, align_bytes=64)
            nc.vector.quantize_mx(out=cd[:].bitcast(FP8X4), scales=sc[:], in_=grouped[(op, k // 2)][:])
            codes[(op, k // 2)] = (cd, sc)

        def load_pw(s):
            if s >= N_STEPS:
                return
            n, m = divmod(s, 8)
            t = raw.tile([P, D], BF16, name="pw", tag="pw", bufs=6)
            nc.sync.dma_start(out=t[:], in_=proto_w[n, P * m : P * (m + 1), :])
            pw_tiles[s] = t

        def mx(j):
            s, h = divmod(j, 2)
            if s >= N_STEPS:
                return
            a_cd, a_sc = codes[("a", s // 2)]
            if j >= TP_FREE and (j - TP_FREE) % 7 < 2:
                x = tps.tile([P, HALF], F32, name="x_tp", tag="tp")
            else:
                x = xps.tile([P, HALF], F32, name="x", tag="x")
            for jj in range(2):
                w_cd, w_sc = codes[("w", 4 * (s // 8) + 2 * h + jj)]
                for g in range(2):
                    a_cols = slice(256 * g + P * (s % 2), 256 * g + P * (s % 2 + 1))
                    w_cols = slice(256 * g, 256 * (g + 1))
                    nc.tensor.matmul_mx(
                        out=x[:, 256 * jj : 256 * (jj + 1)],
                        lhsT=a_cd[:, a_cols].bitcast(FP8X4),
                        lhsT_scale=a_sc[:, a_cols],
                        rhs=w_cd[:, w_cols].bitcast(FP8X4),
                        rhs_scale=w_sc[:, w_cols],
                        start=(g == 0),
                        stop=(g == 1),
                    )
            x_tiles[(s, h)] = x

        def live(t):
            return 0 <= t < N_STEPS

        def pass_over(t, h, func, scale, bias, col):
            junk = work.tile([P, HALF], BF16, name="junk", tag="junk")
            nc.scalar.activation(out=junk[:], in_=x_tiles[(t, h)][:], func=func, scale=scale, bias=bias, accum_out=stat_tiles[t][:, col : col + 1])

        def sum_pass(t, h):
            if not live(t):
                return
            if h == 0:
                stat_tiles[t] = small.tile([P, 6], F32, name="stat", tag="stat")
                pass_over(t, h, ACT.Copy, -1.0 / (D * HALF), 0.0, 0)
            else:
                pass_over(t, h, ACT.Identity, -1.0 / D, stat_tiles[t][:, 0:1], 1)

        def sq_pass(t, h):
            if live(t):
                pass_over(t, h, ACT.Square, 1.0, stat_tiles[t][:, 1:2], 2 + h)

        def var_0(t):
            if live(t):
                nc.scalar.activation(out=stat_tiles[t][:, 4:5], in_=stat_tiles[t][:, 2:3], func=ACT.Copy, scale=1.0 / D, bias=LN_EPS)

        def r_std(t):
            if live(t):
                stat = stat_tiles[t]
                nc.scalar.activation(out=stat[:, 5:6], in_=stat[:, 3:4], func=ACT.Abs_reciprocal_sqrt, scale=1.0 / D, bias=stat[:, 4:5])

        def stats(s):
            sq_pass(s + 1, 0)
            sq_pass(s + 1, 1)
            sum_pass(s + 2, 0)
            var_0(s + 1)
            sum_pass(s + 2, 1)
            r_std(s + 1)

        def c_pe(s):
            if s >= N_STEPS:
                return
            n = s // 8
            c = cps.tile([P, HALF], F32, name="c", tag="c")
            c_tiles[(s, 1)] = c
            nc.tensor.matmul(out=c[:], lhsT=ident_bf[:], rhs=pw_tiles[s][:, HALF:D], start=True, stop=False)
            if s < LATE:
                nc.tensor.matmul(out=c[:], lhsT=sel0[:], rhs=b_bc[:, D * n + HALF : D * (n + 1)], start=False, stop=True)
            else:
                for jj in range(4):
                    col = 8 * n + 4 + jj
                    nc.tensor.matmul(
                        out=c[:, P * jj : P * (jj + 1)],
                        lhsT=b_col[:, col : col + 1].to_broadcast([P, P]),
                        rhs=ident[:],
                        is_transpose=True,
                        start=False,
                        stop=(jj == 3),
                    )

        def c_g(s):
            if s >= N_STEPS:
                return
            n = s // 8
            c = epi.tile([P, HALF], F32, name="cg", tag="cg", bufs=2)
            c_tiles[(s, 0)] = c
            nc.gpsimd.tensor_tensor(out=c[:], in0=pw_tiles[s][:, 0:HALF], in1=b_bc[:, D * n : D * n + HALF], op=ALU.add)

        def epi1(s):
            n = s // 8
            stat = stat_tiles[s]
            rstd = stat[:, 5:6]
            t = epi.tile([P, D], F32, name="t", tag="t")
            for h in range(2):
                cols = slice(HALF * h, HALF * (h + 1))
                nc.vector.scalar_tensor_tensor(out=t[:, cols], in0=x_tiles[(s, h)][:], scalar=stat[:, 1:2], in1=g_bc[:, D * n + HALF * h : D * n + HALF * (h + 1)], op0=ALU.add, op1=ALU.mult)
            t_tiles[s] = (t, rstd)

        def epi2(s, h):
            n, m = divmod(s, 8)
            t, rstd = t_tiles[s]
            if h == 0:
                cy_tiles[s] = epi.tile([P, D], F32, name="cy", tag="cy", bufs=4)
            cy = cy_tiles[s]
            pieces = 2 if (s == N_STEPS - 1 and h == 1) else 1
            width = HALF // pieces
            for q in range(pieces):
                cols = slice(HALF * h + width * q, HALF * h + width * (q + 1))
                nc.vector.scalar_tensor_tensor(out=cy[:, cols], in0=t[:, cols], scalar=rstd, in1=c_tiles[(s, h)][:, width * q : width * (q + 1)], op0=ALU.mult, op1=ALU.add)
                nc.sync.dma_start(out=out[n, P * m : P * (m + 1), cols], in_=cy[:, cols])

        def load_gain_bias(n):
            cols = slice(D * n, D * (n + 1))
            nc.sync.dma_start(out=b_bc[:, cols], in_=pln_b[n, :].partition_broadcast(P))
            nc.sync.dma_start(out=g_bc[:, cols], in_=pln_g[n, :].partition_broadcast(P))

        def keep_warm(count):
            wd = cps.tile([P, count, P], F32, name="warm_ps", tag="c")
            for i in range(count):
                nc.tensor.matmul(out=wd[:, i, :], lhsT=ident[:], rhs=ident[:], start=True, stop=True)

        def item(k):
            load_pairs(k + LOAD_LEAD)
            widen(k + WIDE_LEAD)
            if k >= 2:
                transp(k)
            elif k == 0:
                for op in ("a", "w"):
                    transp(0, (op,))
                    transp(1, (op,))
            if k < WARM_ITEMS:
                keep_warm(2)
            evac(k)

        def late_quantise(k):
            if k <= N_ITEMS:
                quantise("w", k - (1 if k == N_ITEMS else 2))
            quantise("a", k - 3)

        nc.sync.dma_start(out=s_cols[:], in_=pt_w_scale.rearrange("a b (h j i) -> (a b j) h i", h=2, i=4))
        nc.vector.memset(b_rows[:], 0.0)
        load_pairs(0)
        nc.sync.dma_start(out=b_rows[0 : NB * 8, :], in_=pln_b.rearrange("n (j p) -> (n j) p", p=P))
        load_pairs(2)
        load_pairs(4)
        make_identity(nc, ident[:])
        make_identity(nc, ident_bf[:])
        nc.vector.memset(one[:], 1.0)
        nc.vector.memset(sel0[:], 0.0)
        nc.vector.memset(sel0[0:1, :], 1.0)
        nc.scalar.activation(out=warm[:], in_=one[:], func=ACT.Abs_reciprocal_sqrt)
        keep_warm(WARM_START)
        for h in range(2):
            sb = xps.tile([P, 4, P], F32, name="sb", tag="x")
            for i in range(4):
                nc.tensor.transpose(sb[:, i, :], s_cols[:, h, i : i + 1].to_broadcast([P, P]), ident[:])
            nc.scalar.copy(out=scale_bc[:, HALF * h : HALF * (h + 1)].rearrange("p (j i) -> p j i", i=4), in_=sb[:].rearrange("p i j -> p j i"))

        for k in range(WIDE_LEAD):
            widen(k)
        for k in range(ITEM_LEAD):
            item(k)
            late_quantise(k)
            if k == 3:
                bt = tps.tile([P, P], BF16, name="bt", tag="tp")
                nc.tensor.transpose(bt[:], b_rows[:], ident_bf[:])
                nc.scalar.copy(out=b_col[:], in_=bt[:, 0 : NB * 8])
            if k == 6:
                load_gain_bias(0)
                for s in range(4):
                    load_pw(s)
            if k == 9:
                mx(0)
                mx(1)
                stats(-2)
            if k == 10:
                mx(2)
                mx(3)
                stats(-1)
                c_pe(0)
                c_g(0)
            if k == 11:
                mx(4)

        for s in range(N_STEPS):
            k = s + ITEM_LEAD
            load_pw(s + 4)
            load_pairs(k + LOAD_LEAD)
            if s % 8 == 0 and s // 8 + 1 < NB:
                load_gain_bias(s // 8 + 1)
            epi1(s)
            if k < N_ITEMS:
                sq_pass(s + 1, 0)
                sq_pass(s + 1, 1)
                mx(2 * s + 5)
                sum_pass(s + 2, 0)
                var_0(s + 1)
                widen(k + WIDE_LEAD)
                transp(k, ("a",))
                evac(k, ("a",))
                mx(2 * s + 6)
                r_std(s + 1)
                sum_pass(s + 2, 1)
                transp(k, ("w",))
                evac(k, ("w",))
            else:
                mx(2 * s + 7)
                mx(2 * s + 8)
                sum_pass(s + 2, 0)
                if s > N_ITEMS - ITEM_LEAD:
                    r_std(s)
                sq_pass(s + 1, 0)
                sum_pass(s + 2, 1)
                var_0(s + 1)
                sq_pass(s + 1, 1)
            c_pe(s + 1)
            if k == N_ITEMS - 1:
                mx(2 * s + 7)
                mx(2 * s + 8)
            if k != N_ITEMS:
                late_quantise(k)
            epi2(s, 0)
            c_g(s + 1)
            epi2(s, 1)
            if k == N_ITEMS:
                late_quantise(k)
